import numpy as np
import ml_dtypes


def mxq(x, axis, fmt="e4m3"):
    dtype, down = {"e4m3": (ml_dtypes.float8_e4m3fn, 7), "e5m2": (ml_dtypes.float8_e5m2, 14)}[fmt]
    v = np.moveaxis(np.asarray(x, np.float32).astype(ml_dtypes.bfloat16).astype(np.float64), axis, -1)
    blocks = v.reshape(v.shape[:-1] + (-1, 32))
    amax = np.abs(blocks).max(-1, keepdims=True)
    byte = np.maximum(np.where(amax > 0, np.frexp(amax)[1] - 1 + 127, 0) - down, 1)
    scale = np.exp2(byte - 127.0)
    codes = (blocks / scale).astype(np.float32).astype(dtype).astype(np.float64)
    return np.moveaxis((codes * scale).reshape(v.shape), -1, axis)


WIDE = False


def mx_kscale(k):
    if not WIDE:
        return np.ones(k)
    levels = np.array([10, -10, 5, -5, 0])
    a = np.random.permutation(np.resize(levels, k // 512 * 4)).reshape(k // 512, 4)
    idx = np.arange(k)
    return np.exp2(a[idx // 512, idx % 128 // 32])


BF16 = ml_dtypes.bfloat16


def bf(x):
    return np.asarray(x, np.float32).astype(BF16)


def f64(x):
    return np.asarray(x).astype(np.float64)


B, C, HH, WW = 32, 512, 16, 16
N = HH * WW


def setup_inputs():
    s, t = mx_kscale(C), mx_kscale(C)
    return {"x": bf(np.random.standard_normal((B, C, HH, WW)) * s[None, :, None, None]),
            "Wq": bf(np.random.standard_normal((C, C)) * 1.4 / np.sqrt(C) * t[:, None] / s[None, :]),
            "bq": bf(np.random.standard_normal(C) * 0.2 * t),
            "k": bf(np.random.standard_normal((B, N, C)) * 1.4 / t)}


def reference(x, Wq, bq, k):
    xt = f64(x).reshape(B, C, N)
    q = (mxq(xt, 1, "e4m3").transpose(0, 2, 1) @ mxq(f64(Wq), 1, "e4m3").T) + f64(bq)
    scores = mxq(q / np.sqrt(C), 2, "e4m3") @ mxq(f64(k), 2, "e4m3").transpose(0, 2, 1)
    e = np.exp(scores - scores.max(-1, keepdims=True))
    return e / e.sum(-1, keepdims=True)

@@ -1,0 +1,307 @@
+import math
+from contextlib import ExitStack
+
+import concourse.mybir as mybir
+from concourse.masks import make_identity
+
+F32 = mybir.dt.float32
+BF16 = mybir.dt.bfloat16
+U32 = mybir.dt.uint32
+U8 = mybir.dt.uint8
+FP8X4 = mybir.dt.float8_e4m3fn_x4
+ACT = mybir.ActivationFunctionType
+ALU = mybir.AluOpType
+
+P = 128
+PACK = 4
+BATCHES = 32
+CHANNELS = P * PACK
+TOKENS = 256
+KEYS = 256
+HALVES = TOKENS // P
+PAIR = 2
+STEPS = BATCHES // PAIR
+COLS = PAIR * TOKENS
+ROW_TILES = PAIR * HALVES
+RUN = 4
+Q_SCALE = 1.0 / math.sqrt(CHANNELS)
+
+PROJECT_LAG = 1
+SCORE_LAG = 2
+SOFTMAX_LAG = 3
+NORM_LAG = 4
+LOOKAHEAD = 3
+
+FLOPS = 2 * BATCHES * TOKENS * CHANNELS * CHANNELS + 2 * BATCHES * TOKENS * KEYS * CHANNELS
+
+
+def tile_visionattention_pa_t_kernel(tc, x, Wq, bq, k, out):
+    nc = tc.nc
+    with ExitStack() as ctx:
+        const = ctx.enter_context(tc.tile_pool(name="const", bufs=1))
+        rows = ctx.enter_context(tc.tile_pool(name="rows", bufs=LOOKAHEAD + 1))
+        work = ctx.enter_context(tc.tile_pool(name="work", bufs=2))
+        handed = ctx.enter_context(tc.tile_pool(name="handed", bufs=3))
+        t_psum = ctx.enter_context(tc.psum_pool(name="t_psum", bufs=2))
+        q_psum = ctx.enter_context(tc.psum_pool(name="q_psum", bufs=PACK))
+        s_psum = ctx.enter_context(tc.psum_pool(name="s_psum", bufs=PAIR))
+        ctx.enter_context(tc.manual_schedule())
+
+        x_rows, k_rows = {}, {}
+        x_grouped, k_grouped, q_planes, q_grouped = {}, {}, {}, {}
+        x_mx, k_mx, q_mx = {}, {}, {}
+        scores, neg_max, row_sum, inv_sum, probs = {}, {}, {}, {}, {}
+
+        def quantise(grouped, operand):
+            words = handed.tile([P, COLS], U32, tag=operand + "_words", align_bytes=64)
+            scales = handed.tile([P, COLS], U8, tag=operand + "_scales", align_bytes=64)
+            nc.vector.quantize_mx(out=words[:].bitcast(FP8X4), scales=scales[:], in_=grouped[:])
+            return words, scales
+
+        def multiply(acc, stationary, s_cols, moving, m_cols):
+            nc.tensor.matmul_mx(
+                out=acc,
+                lhsT=stationary[0][:, s_cols].bitcast(FP8X4),
+                lhsT_scale=stationary[1][:, s_cols],
+                rhs=moving[0][:, m_cols].bitcast(FP8X4),
+                rhs_scale=moving[1][:, m_cols],
+                start=True,
+                stop=True,
+            )
+
+
+        def load(i):
+            batches = slice(PAIR * i, PAIR * (i + 1))
+            x_tile = rows.tile([P, PAIR, PACK, TOKENS], BF16)
+            nc.sync.dma_start(
+                out=x_tile[:].rearrange("p b j n -> p b (j n)"),
+                in_=x[batches].rearrange("b (p j) h w -> p b (j h w)", j=PACK),
+            )
+            k_tile = rows.tile([P, ROW_TILES * CHANNELS], BF16)
+            nc.sync.dma_start(
+                out=k_tile[:].rearrange("r (g c) -> r g c", g=ROW_TILES),
+                in_=k[batches].rearrange("b (h r) c -> r (b h) c", r=P),
+            )
+            x_rows[i], k_rows[i] = x_tile, k_tile
+
+        def regroup_x(i):
+            x_side = work.tile([P, COLS * PACK], BF16, align_bytes=64)
+            nc.vector.tensor_copy(
+                out=x_side[:].rearrange("p (b c i j) -> p b c j i", b=PAIR, i=RUN, j=PACK),
+                in_=x_rows[i][:].rearrange("p b j (c i) -> p b c j i", i=RUN),
+            )
+            x_grouped[i] = x_side
+
+        def quantise_x(i):
+            x_mx[i] = quantise(x_grouped[i], "x")
+
+        def transpose_k(i):
+            k_words = k_rows[i][:].bitcast(F32).rearrange("r (g w) -> r g w", g=ROW_TILES)
+            k_side = handed.tile([P, COLS * PACK], BF16, align_bytes=64)
+            k_pairs = k_side[:].bitcast(F32).rearrange("p (b h r u) -> p b h r u", b=PAIR, h=HALVES, u=2)
+            banks = []
+            for b in range(PAIR):
+                bank = t_psum.tile([P, HALVES, 2, P], F32)
+                for h in range(HALVES):
+                    for u in range(2):
+                        nc.tensor.transpose(
+                            out=bank[:, h, u, :],
+                            in_=k_words[:, b * HALVES + h, u * P : (u + 1) * P],
+                            identity=ident[:],
+                        )
+                banks.append(bank)
+            for b in range(PAIR):
+                nc.scalar.copy(
+                    out=k_pairs[:, b], in_=banks[b][:].rearrange("p h u r -> p h r u")
+                )
+            k_grouped[i] = k_side
+
+        def quantise_k(i):
+            k_mx[i] = quantise(k_grouped[i], "k")
+
+        def project(i):
+            planes = handed.tile([P, PACK, COLS], BF16)
+            accs = []
+            for t in range(PACK):
+                acc = q_psum.tile([P, COLS], F32)
+                multiply(acc[:], w_mx, slice(t * P, (t + 1) * P), x_mx[i], slice(0, COLS))
+                accs.append(acc)
+            for t in range(PACK):
+                nc.scalar.activation(
+                    out=planes[:, t, :],
+                    in_=accs[t][:],
+                    func=ACT.Identity,
+                    bias=bias_scaled[:, t : t + 1],
+                    scale=Q_SCALE,
+                )
+            q_planes[i] = planes
+
+        def regroup_q(i):
+            q_side = work.tile([P, COLS * PACK], BF16, align_bytes=64)
+            nc.vector.tensor_copy(
+                out=q_side[:].rearrange("p (c i t) -> p c t i", i=RUN, t=PACK),
+                in_=q_planes[i][:].rearrange("p t (c i) -> p c t i", i=RUN),
+            )
+            q_grouped[i] = q_side
+
+        def quantise_q(i):
+            q_mx[i] = quantise(q_grouped[i], "q")
+
+        def score(i):
+            scores[i] = []
+            for b in range(PAIR):
+                bank = s_psum.tile([P, HALVES, KEYS], F32)
+                for h in range(HALVES):
+                    first = b * TOKENS + h * P
+                    multiply(
+                        bank[:, h, :],
+                        q_mx[i],
+                        slice(first, first + P),
+                        k_mx[i],
+                        slice(b * KEYS, (b + 1) * KEYS),
+                    )
+                scores[i].append(bank)
+
+        def row_maxima(i):
+            maxima = handed.tile([P, PAIR, HALVES], F32)
+            for b in range(PAIR):
+                nc.vector.tensor_reduce(
+                    out=maxima[:, b, :],
+                    in_=scores[i][b][:],
+                    axis=mybir.AxisListType.X,
+                    op=ALU.max,
+                    negate=True,
+                )
+            neg_max[i] = maxima
+
+        def exponentials(i):
+            e = handed.tile([P, PAIR, HALVES, KEYS], F32)
+            sums = handed.tile([P, PAIR, HALVES], F32)
+            for b in range(PAIR):
+                for h in range(HALVES):
+                    nc.scalar.activation(
+                        out=e[:, b, h, :],
+                        in_=scores[i][b][:, h, :],
+                        func=ACT.Exp,
+                        bias=neg_max[i][:, b, h : h + 1],
+                        scale=1.0,
+                        accum_out=sums[:, b, h : h + 1],
+                    )
+            probs[i], row_sum[i] = e, sums
+
+        def invert_sums(i):
+            inverse = handed.tile([P, PAIR, HALVES], F32)
+            nc.vector.reciprocal(out=inverse[:], in_=row_sum[i][:])
+            inv_sum[i] = inverse
+
+        def normalise_on_scalar(i):
+            for b in range(PAIR):
+                nc.scalar.activation(
+                    out=probs[i][:, b, 1, :],
+                    in_=probs[i][:, b, 1, :],
+                    func=ACT.Copy,
+                    scale=inv_sum[i][:, b, 1:2],
+                )
+
+        def normalise_on_vector(i):
+            for b in range(PAIR):
+                nc.vector.tensor_scalar(
+                    out=probs[i][:, b, 0, :],
+                    in0=probs[i][:, b, 0, :],
+                    scalar1=inv_sum[i][:, b, 0:1],
+                    scalar2=None,
+                    op0=ALU.mult,
+                )
+
+        def store(i):
+            nc.sync.dma_start(
+                out=out[PAIR * i : PAIR * (i + 1)].rearrange("b (h r) m -> r (b h) m", r=P),
+                in_=probs[i][:].rearrange("r b h m -> r (b h) m"),
+            )
+
+
+        w_rows = const.tile([P, PACK * CHANNELS], BF16)
+        nc.sync.dma_start(
+            out=w_rows[:].rearrange("r (u ec) -> r u ec", u=2),
+            in_=Wq.rearrange("(u r e) c -> r u (e c)", u=2, e=2),
+        )
+        for i in range(LOOKAHEAD):
+            load(i)
+        bias_bf = const.tile([P, PACK], BF16)
+        nc.scalar.dma_start(
+            out=bias_bf[:].rearrange("r (u e) -> r u e", u=2),
+            in_=bq.rearrange("(u r e) -> r u e", u=2, e=2),
+        )
+
+        warm = const.tile([P, 1], F32)
+        nc.vector.memset(warm[:], 0.0)
+        nc.scalar.activation(out=warm[:], in_=warm[:], func=ACT.Exp)
+
+        ident = const.tile([P, P], F32)
+        make_identity(nc, ident[:])
+
+        bias_scaled = const.tile([P, PACK], F32)
+        nc.vector.tensor_scalar(
+            out=bias_scaled[:], in0=bias_bf[:], scalar1=Q_SCALE, scalar2=None, op0=ALU.mult
+        )
+
+        w_words = w_rows[:].bitcast(F32).rearrange("r (t p v) -> r t v p", t=PACK, v=2)
+        w_side = const.tile([P, PACK * P * PACK], BF16, align_bytes=64)
+        w_pairs = w_side[:].bitcast(F32).rearrange("p (t r v) -> p t r v", t=PACK, v=2)
+        w_banks = []
+        for half in range(2):
+            bank = t_psum.tile([P, 2, 2, P], F32)
+            for t in range(2):
+                for v in range(2):
+                    nc.tensor.transpose(
+                        out=bank[:, t, v, :], in_=w_words[:, 2 * half + t, v, :], identity=ident[:]
+                    )
+            w_banks.append(bank)
+        for half in range(2):
+            nc.scalar.copy(
+                out=w_pairs[:, 2 * half : 2 * half + 2, :, :],
+                in_=w_banks[half][:].rearrange("p t v r -> p t r v"),
+            )
+        w_words_mx = const.tile([P, CHANNELS], U32, align_bytes=64)
+        w_scales = const.tile([P, CHANNELS], U8, align_bytes=64)
+        nc.vector.quantize_mx(
+            out=w_words_mx[:].bitcast(FP8X4),
+            scales=w_scales[:],
+            in_=w_side[:],
+        )
+        w_mx = (w_words_mx, w_scales)
+
+
+        def due(i):
+            return 0 <= i < STEPS
+
+        for turn in range(STEPS + NORM_LAG):
+            if due(turn + LOOKAHEAD):
+                load(turn + LOOKAHEAD)
+            if due(turn - SOFTMAX_LAG):
+                row_maxima(turn - SOFTMAX_LAG)
+            if due(turn - NORM_LAG):
+                invert_sums(turn - NORM_LAG)
+            if due(turn):
+                transpose_k(turn)
+            if due(turn - SOFTMAX_LAG):
+                exponentials(turn - SOFTMAX_LAG)
+            if due(turn - NORM_LAG):
+                normalise_on_scalar(turn - NORM_LAG)
+            if due(turn - SCORE_LAG):
+                regroup_q(turn - SCORE_LAG)
+            if due(turn):
+                regroup_x(turn)
+            if due(turn - SCORE_LAG):
+                quantise_q(turn - SCORE_LAG)
+            if due(turn - PROJECT_LAG):
+                quantise_k(turn - PROJECT_LAG)
+            if due(turn):
+                quantise_x(turn)
+            if due(turn - PROJECT_LAG):
+                project(turn - PROJECT_LAG)
+            if due(turn - SCORE_LAG):
+                score(turn - SCORE_LAG)
+            if due(turn - NORM_LAG):
+                normalise_on_vector(turn - NORM_LAG)
+                store(turn - NORM_LAG)

@@ -40,17 +40,17 @@ def tile_visionattention_pa_t_kernel(tc, x, Wq, bq, k, out):
     with ExitStack() as ctx:
         const = ctx.enter_context(tc.tile_pool(name="const", bufs=1))
         rows = ctx.enter_context(tc.tile_pool(name="rows", bufs=LOOKAHEAD + 1))
-        work = ctx.enter_context(tc.tile_pool(name="work", bufs=2))
         handed = ctx.enter_context(tc.tile_pool(name="handed", bufs=3))
+        results = ctx.enter_context(tc.tile_pool(name="results", bufs=4))
         t_psum = ctx.enter_context(tc.psum_pool(name="t_psum", bufs=2))
-        q_psum = ctx.enter_context(tc.psum_pool(name="q_psum", bufs=PACK))
+        q_psum = ctx.enter_context(tc.psum_pool(name="q_psum", bufs=ROW_TILES))
         s_psum = ctx.enter_context(tc.psum_pool(name="s_psum", bufs=PAIR))
         ctx.enter_context(tc.manual_schedule())
 
         x_rows, k_rows = {}, {}
-        x_grouped, k_grouped, q_planes, q_grouped = {}, {}, {}, {}
+        x_grouped, k_grouped, q_grouped = {}, {}, {}
         x_mx, k_mx, q_mx = {}, {}, {}
-        scores, neg_max, row_sum, inv_sum, probs = {}, {}, {}, {}, {}
+        q_banks, scores, neg_max, row_sum, inv_sum, probs = {}, {}, {}, {}, {}, {}
 
         def quantise(grouped, operand):
             words = handed.tile([P, COLS], U32, tag=operand + "_words", align_bytes=64)
@@ -85,15 +85,13 @@ def tile_visionattention_pa_t_kernel(tc, x, Wq, bq, k, out):
             x_rows[i], k_rows[i] = x_tile, k_tile
 
         def regroup_x(i):
-            x_side = work.tile([P, COLS * PACK], BF16, align_bytes=64)
-            nc.vector.tensor_copy(
-                out=x_side[:].rearrange("p (b c i j) -> p b c j i", b=PAIR, i=RUN, j=PACK),
-                in_=x_rows[i][:].rearrange("p b j (c i) -> p b c j i", i=RUN),
-            )
+            x_side = handed.tile([P, COLS * PACK], BF16, align_bytes=64)
+            by_batch = x_side[:].rearrange("p (b c i j) -> p b c j i", b=PAIR, i=RUN, j=PACK)
+            for b in range(PAIR):
+                nc.scalar.copy(
+                    out=by_batch[:, b], in_=x_rows[i][:, b].rearrange("p j (c i) -> p c j i", i=RUN)
+                )
             x_grouped[i] = x_side
-
-        def quantise_x(i):
-            x_mx[i] = quantise(x_grouped[i], "x")
 
         def transpose_k(i):
             k_words = k_rows[i][:].bitcast(F32).rearrange("r (g w) -> r g w", g=ROW_TILES)
@@ -111,41 +109,32 @@ def tile_visionattention_pa_t_kernel(tc, x, Wq, bq, k, out):
                         )
                 banks.append(bank)
             for b in range(PAIR):
-                nc.scalar.copy(
-                    out=k_pairs[:, b], in_=banks[b][:].rearrange("p h u r -> p h r u")
-                )
+                nc.scalar.copy(out=k_pairs[:, b], in_=banks[b][:].rearrange("p h u r -> p h r u"))
             k_grouped[i] = k_side
 
-        def quantise_k(i):
-            k_mx[i] = quantise(k_grouped[i], "k")
-
         def project(i):
-            planes = handed.tile([P, PACK, COLS], BF16)
-            accs = []
-            for t in range(PACK):
-                acc = q_psum.tile([P, COLS], F32)
-                multiply(acc[:], w_mx, slice(t * P, (t + 1) * P), x_mx[i], slice(0, COLS))
-                accs.append(acc)
-            for t in range(PACK):
-                nc.scalar.activation(
-                    out=planes[:, t, :],
-                    in_=accs[t][:],
-                    func=ACT.Identity,
-                    bias=bias_scaled[:, t : t + 1],
-                    scale=Q_SCALE,
+            q_banks[i] = []
+            for g in range(ROW_TILES):
+                bank = q_psum.tile([P, PACK, P], F32)
+                for t in range(PACK):
+                    multiply(
+                        bank[:, t, :], w_mx, slice(t * P, (t + 1) * P), x_mx[i], slice(g * P, (g + 1) * P)
+                    )
+                q_banks[i].append(bank)
+
+        def q_out_of_psum(i):
+            q_side = handed.tile([P, COLS * PACK], BF16, align_bytes=64)
+            by_tile = q_side[:].rearrange("p (g n t) -> p g n t", g=ROW_TILES, t=PACK)
+            for g in range(ROW_TILES):
+                nc.vector.scalar_tensor_tensor(
+                    out=by_tile[:, g],
+                    in0=q_banks[i][g][:].rearrange("p t n -> p n t"),
+                    scalar=Q_SCALE,
+                    in1=bias_scaled[:].unsqueeze(1).to_broadcast([P, P, PACK]),
+                    op0=ALU.mult,
+                    op1=ALU.add,
                 )
-            q_planes[i] = planes
-
-        def regroup_q(i):
-            q_side = work.tile([P, COLS * PACK], BF16, align_bytes=64)
-            nc.vector.tensor_copy(
-                out=q_side[:].rearrange("p (c i t) -> p c t i", i=RUN, t=PACK),
-                in_=q_planes[i][:].rearrange("p t (c i) -> p c t i", i=RUN),
-            )
             q_grouped[i] = q_side
-
-        def quantise_q(i):
-            q_mx[i] = quantise(q_grouped[i], "q")
 
         def score(i):
             scores[i] = []
@@ -175,8 +164,8 @@ def tile_visionattention_pa_t_kernel(tc, x, Wq, bq, k, out):
             neg_max[i] = maxima
 
         def exponentials(i):
-            e = handed.tile([P, PAIR, HALVES, KEYS], F32)
-            sums = handed.tile([P, PAIR, HALVES], F32)
+            e = results.tile([P, PAIR, HALVES, KEYS], F32)
+            sums = results.tile([P, PAIR, HALVES], F32)
             for b in range(PAIR):
                 for h in range(HALVES):
                     nc.scalar.activation(
@@ -190,34 +179,24 @@ def tile_visionattention_pa_t_kernel(tc, x, Wq, bq, k, out):
             probs[i], row_sum[i] = e, sums
 
         def invert_sums(i):
-            inverse = handed.tile([P, PAIR, HALVES], F32)
+            inverse = results.tile([P, PAIR, HALVES], F32)
             nc.vector.reciprocal(out=inverse[:], in_=row_sum[i][:])
             inv_sum[i] = inverse
 
-        def normalise_on_scalar(i):
+        def normalise_and_store(i):
             for b in range(PAIR):
-                nc.scalar.activation(
-                    out=probs[i][:, b, 1, :],
-                    in_=probs[i][:, b, 1, :],
-                    func=ACT.Copy,
-                    scale=inv_sum[i][:, b, 1:2],
+                for h in range(HALVES):
+                    nc.gpsimd.tensor_scalar(
+                        out=probs[i][:, b, h, :],
+                        in0=probs[i][:, b, h, :],
+                        scalar1=inv_sum[i][:, b, h : h + 1],
+                        scalar2=0.0,
+                        op0=ALU.mult,
+                        op1=ALU.add,
+                    )
+                nc.sync.dma_start(
+                    out=out[PAIR * i + b].rearrange("(h r) m -> r h m", r=P), in_=probs[i][:, b]
                 )
-
-        def normalise_on_vector(i):
-            for b in range(PAIR):
-                nc.vector.tensor_scalar(
-                    out=probs[i][:, b, 0, :],
-                    in0=probs[i][:, b, 0, :],
-                    scalar1=inv_sum[i][:, b, 0:1],
-                    scalar2=None,
-                    op0=ALU.mult,
-                )
-
-        def store(i):
-            nc.sync.dma_start(
-                out=out[PAIR * i : PAIR * (i + 1)].rearrange("b (h r) m -> r (b h) m", r=P),
-                in_=probs[i][:].rearrange("r b h m -> r (b h) m"),
-            )
 
 
         w_rows = const.tile([P, PACK * CHANNELS], BF16)
@@ -258,17 +237,13 @@ def tile_visionattention_pa_t_kernel(tc, x, Wq, bq, k, out):
                     )
             w_banks.append(bank)
         for half in range(2):
-            nc.scalar.copy(
+            nc.vector.tensor_copy(
                 out=w_pairs[:, 2 * half : 2 * half + 2, :, :],
                 in_=w_banks[half][:].rearrange("p t v r -> p t r v"),
             )
         w_words_mx = const.tile([P, CHANNELS], U32, align_bytes=64)
         w_scales = const.tile([P, CHANNELS], U8, align_bytes=64)
-        nc.vector.quantize_mx(
-            out=w_words_mx[:].bitcast(FP8X4),
-            scales=w_scales[:],
-            in_=w_side[:],
-        )
+        nc.vector.quantize_mx(out=w_words_mx[:].bitcast(FP8X4), scales=w_scales[:], in_=w_side[:])
         w_mx = (w_words_mx, w_scales)
 
 
@@ -278,30 +253,24 @@ def tile_visionattention_pa_t_kernel(tc, x, Wq, bq, k, out):
         for turn in range(STEPS + NORM_LAG):
             if due(turn + LOOKAHEAD):
                 load(turn + LOOKAHEAD)
+            if due(turn):
+                regroup_x(turn)
+                transpose_k(turn)
+            if due(turn - SCORE_LAG):
+                q_out_of_psum(turn - SCORE_LAG)
+            if due(turn - PROJECT_LAG):
+                x_mx[turn - PROJECT_LAG] = quantise(x_grouped[turn - PROJECT_LAG], "x")
+                project(turn - PROJECT_LAG)
             if due(turn - SOFTMAX_LAG):
                 row_maxima(turn - SOFTMAX_LAG)
             if due(turn - NORM_LAG):
                 invert_sums(turn - NORM_LAG)
-            if due(turn):
-                transpose_k(turn)
             if due(turn - SOFTMAX_LAG):
                 exponentials(turn - SOFTMAX_LAG)
             if due(turn - NORM_LAG):
-                normalise_on_scalar(turn - NORM_LAG)
-            if due(turn - SCORE_LAG):
-                regroup_q(turn - SCORE_LAG)
-            if due(turn):
-                regroup_x(turn)
-            if due(turn - SCORE_LAG):
-                quantise_q(turn - SCORE_LAG)
+                normalise_and_store(turn - NORM_LAG)
             if due(turn - PROJECT_LAG):
-                quantise_k(turn - PROJECT_LAG)
-            if due(turn):
-                quantise_x(turn)
-            if due(turn - PROJECT_LAG):
-                project(turn - PROJECT_LAG)
+                k_mx[turn - PROJECT_LAG] = quantise(k_grouped[turn - PROJECT_LAG], "k")
             if due(turn - SCORE_LAG):
+                q_mx[turn - SCORE_LAG] = quantise(q_grouped[turn - SCORE_LAG], "q")
                 score(turn - SCORE_LAG)
-            if due(turn - NORM_LAG):
-                normalise_on_vector(turn - NORM_LAG)
-                store(turn - NORM_LAG)

@@ -253,24 +253,23 @@ def tile_visionattention_pa_t_kernel(tc, x, Wq, bq, k, out):
         for turn in range(STEPS + NORM_LAG):
             if due(turn + LOOKAHEAD):
                 load(turn + LOOKAHEAD)
+            if due(turn - NORM_LAG):
+                invert_sums(turn - NORM_LAG)
+                normalise_and_store(turn - NORM_LAG)
             if due(turn):
                 regroup_x(turn)
                 transpose_k(turn)
             if due(turn - SCORE_LAG):
                 q_out_of_psum(turn - SCORE_LAG)
+            if due(turn - SOFTMAX_LAG):
+                row_maxima(turn - SOFTMAX_LAG)
+                exponentials(turn - SOFTMAX_LAG)
             if due(turn - PROJECT_LAG):
                 x_mx[turn - PROJECT_LAG] = quantise(x_grouped[turn - PROJECT_LAG], "x")
                 project(turn - PROJECT_LAG)
-            if due(turn - SOFTMAX_LAG):
-                row_maxima(turn - SOFTMAX_LAG)
-            if due(turn - NORM_LAG):
-                invert_sums(turn - NORM_LAG)
-            if due(turn - SOFTMAX_LAG):
-                exponentials(turn - SOFTMAX_LAG)
-            if due(turn - NORM_LAG):
-                normalise_and_store(turn - NORM_LAG)
+            if due(turn - SCORE_LAG):
+                q_mx[turn - SCORE_LAG] = quantise(q_grouped[turn - SCORE_LAG], "q")
             if due(turn - PROJECT_LAG):
                 k_mx[turn - PROJECT_LAG] = quantise(k_grouped[turn - PROJECT_LAG], "k")
             if due(turn - SCORE_LAG):
-                q_mx[turn - SCORE_LAG] = quantise(q_grouped[turn - SCORE_LAG], "q")
                 score(turn - SCORE_LAG)

@@ -39,7 +39,7 @@ def tile_visionattention_pa_t_kernel(tc, x, Wq, bq, k, out):
     nc = tc.nc
     with ExitStack() as ctx:
         const = ctx.enter_context(tc.tile_pool(name="const", bufs=1))
-        rows = ctx.enter_context(tc.tile_pool(name="rows", bufs=LOOKAHEAD + 1))
+        rows = ctx.enter_context(tc.tile_pool(name="rows", bufs=LOOKAHEAD + 1 + PROJECT_LAG))
         handed = ctx.enter_context(tc.tile_pool(name="handed", bufs=3))
         results = ctx.enter_context(tc.tile_pool(name="results", bufs=4))
         t_psum = ctx.enter_context(tc.psum_pool(name="t_psum", bufs=2))
@@ -73,10 +73,11 @@ def tile_visionattention_pa_t_kernel(tc, x, Wq, bq, k, out):
         def load(i):
             batches = slice(PAIR * i, PAIR * (i + 1))
             x_tile = rows.tile([P, PAIR, PACK, TOKENS], BF16)
-            nc.sync.dma_start(
-                out=x_tile[:].rearrange("p b j n -> p b (j n)"),
-                in_=x[batches].rearrange("b (p j) h w -> p b (j h w)", j=PACK),
-            )
+            for b in range(PAIR):
+                nc.sync.dma_start(
+                    out=x_tile[:, b].rearrange("p j n -> p (j n)"),
+                    in_=x[PAIR * i + b].rearrange("(p j) h w -> p (j h w)", j=PACK),
+                )
             k_tile = rows.tile([P, ROW_TILES * CHANNELS], BF16)
             nc.sync.dma_start(
                 out=k_tile[:].rearrange("r (g c) -> r g c", g=ROW_TILES),
@@ -184,9 +185,10 @@ def tile_visionattention_pa_t_kernel(tc, x, Wq, bq, k, out):
             inv_sum[i] = inverse
 
         def normalise_and_store(i):
+            engine = nc.vector if i == STEPS - 1 else nc.gpsimd
             for b in range(PAIR):
                 for h in range(HALVES):
-                    nc.gpsimd.tensor_scalar(
+                    engine.tensor_scalar(
                         out=probs[i][:, b, h, :],
                         in0=probs[i][:, b, h, :],
                         scalar1=inv_sum[i][:, b, h : h + 1],
@@ -200,10 +202,11 @@ def tile_visionattention_pa_t_kernel(tc, x, Wq, bq, k, out):
 
 
         w_rows = const.tile([P, PACK * CHANNELS], BF16)
-        nc.sync.dma_start(
-            out=w_rows[:].rearrange("r (u ec) -> r u ec", u=2),
-            in_=Wq.rearrange("(u r e) c -> r u (e c)", u=2, e=2),
-        )
+        for u in range(2):
+            nc.sync.dma_start(
+                out=w_rows[:].rearrange("r (u ec) -> r u ec", u=2)[:, u],
+                in_=Wq.rearrange("(u r e) c -> u r (e c)", u=2, e=2)[u],
+            )
         for i in range(LOOKAHEAD):
             load(i)
         bias_bf = const.tile([P, PACK], BF16)
@@ -258,7 +261,8 @@ def tile_visionattention_pa_t_kernel(tc, x, Wq, bq, k, out):
                 normalise_and_store(turn - NORM_LAG)
             if due(turn):
                 regroup_x(turn)
-                transpose_k(turn)
+            if due(turn - PROJECT_LAG):
+                transpose_k(turn - PROJECT_LAG)
             if due(turn - SCORE_LAG):
                 q_out_of_psum(turn - SCORE_LAG)
             if due(turn - SOFTMAX_LAG):
@@ -268,8 +272,6 @@ def tile_visionattention_pa_t_kernel(tc, x, Wq, bq, k, out):
                 x_mx[turn - PROJECT_LAG] = quantise(x_grouped[turn - PROJECT_LAG], "x")
                 project(turn - PROJECT_LAG)
             if due(turn - SCORE_LAG):
+                k_mx[turn - SCORE_LAG] = quantise(k_grouped[turn - SCORE_LAG], "k")
                 q_mx[turn - SCORE_LAG] = quantise(q_grouped[turn - SCORE_LAG], "q")
-            if due(turn - PROJECT_LAG):
-                k_mx[turn - PROJECT_LAG] = quantise(k_grouped[turn - PROJECT_LAG], "k")
-            if due(turn - SCORE_LAG):
                 score(turn - SCORE_LAG)

import math
from contextlib import ExitStack

import concourse.mybir as mybir
from concourse.masks import make_identity

F32 = mybir.dt.float32
BF16 = mybir.dt.bfloat16
U32 = mybir.dt.uint32
U8 = mybir.dt.uint8
FP8X4 = mybir.dt.float8_e4m3fn_x4
ACT = mybir.ActivationFunctionType
ALU = mybir.AluOpType

P = 128
PACK = 4
BATCHES = 32
CHANNELS = P * PACK
TOKENS = 256
KEYS = 256
HALVES = TOKENS // P
PAIR = 2
STEPS = BATCHES // PAIR
COLS = PAIR * TOKENS
ROW_TILES = PAIR * HALVES
RUN = 4
Q_SCALE = 1.0 / math.sqrt(CHANNELS)

PROJECT_LAG = 1
SCORE_LAG = 2
SOFTMAX_LAG = 3
NORM_LAG = 4
LOOKAHEAD = 3

FLOPS = 2 * BATCHES * TOKENS * CHANNELS * CHANNELS + 2 * BATCHES * TOKENS * KEYS * CHANNELS


def tile_visionattention_pa_t_kernel(tc, x, Wq, bq, k, out):
    nc = tc.nc
    with ExitStack() as ctx:
        const = ctx.enter_context(tc.tile_pool(name="const", bufs=1))
        rows = ctx.enter_context(tc.tile_pool(name="rows", bufs=LOOKAHEAD + 1 + PROJECT_LAG))
        handed = ctx.enter_context(tc.tile_pool(name="handed", bufs=3))
        results = ctx.enter_context(tc.tile_pool(name="results", bufs=4))
        t_psum = ctx.enter_context(tc.psum_pool(name="t_psum", bufs=2))
        q_psum = ctx.enter_context(tc.psum_pool(name="q_psum", bufs=ROW_TILES))
        s_psum = ctx.enter_context(tc.psum_pool(name="s_psum", bufs=PAIR))
        ctx.enter_context(tc.manual_schedule())

        x_rows, k_rows = {}, {}
        x_grouped, k_grouped, q_grouped = {}, {}, {}
        x_mx, k_mx, q_mx = {}, {}, {}
        q_banks, scores, neg_max, row_sum, inv_sum, probs = {}, {}, {}, {}, {}, {}

        def quantise(grouped, operand):
            words = handed.tile([P, COLS], U32, tag=operand + "_words", align_bytes=64)
            scales = handed.tile([P, COLS], U8, tag=operand + "_scales", align_bytes=64)
            nc.vector.quantize_mx(out=words[:].bitcast(FP8X4), scales=scales[:], in_=grouped[:])
            return words, scales

        def multiply(acc, stationary, s_cols, moving, m_cols):
            nc.tensor.matmul_mx(
                out=acc,
                lhsT=stationary[0][:, s_cols].bitcast(FP8X4),
                lhsT_scale=stationary[1][:, s_cols],
                rhs=moving[0][:, m_cols].bitcast(FP8X4),
                rhs_scale=moving[1][:, m_cols],
                start=True,
                stop=True,
            )


        def load(i):
            batches = slice(PAIR * i, PAIR * (i + 1))
            x_tile = rows.tile([P, PAIR, PACK, TOKENS], BF16)
            for b in range(PAIR):
                nc.sync.dma_start(
                    out=x_tile[:, b].rearrange("p j n -> p (j n)"),
                    in_=x[PAIR * i + b].rearrange("(p j) h w -> p (j h w)", j=PACK),
                )
            k_tile = rows.tile([P, ROW_TILES * CHANNELS], BF16)
            nc.sync.dma_start(
                out=k_tile[:].rearrange("r (g c) -> r g c", g=ROW_TILES),
                in_=k[batches].rearrange("b (h r) c -> r (b h) c", r=P),
            )
            x_rows[i], k_rows[i] = x_tile, k_tile

        def regroup_x(i):
            x_side = handed.tile([P, COLS * PACK], BF16, align_bytes=64)
            by_batch = x_side[:].rearrange("p (b c i j) -> p b c j i", b=PAIR, i=RUN, j=PACK)
            for b in range(PAIR):
                nc.scalar.copy(
                    out=by_batch[:, b], in_=x_rows[i][:, b].rearrange("p j (c i) -> p c j i", i=RUN)
                )
            x_grouped[i] = x_side

        def transpose_k(i):
            k_words = k_rows[i][:].bitcast(F32).rearrange("r (g w) -> r g w", g=ROW_TILES)
            k_side = handed.tile([P, COLS * PACK], BF16, align_bytes=64)
            k_pairs = k_side[:].bitcast(F32).rearrange("p (b h r u) -> p b h r u", b=PAIR, h=HALVES, u=2)
            banks = []
            for b in range(PAIR):
                bank = t_psum.tile([P, HALVES, 2, P], F32)
                for h in range(HALVES):
                    for u in range(2):
                        nc.tensor.transpose(
                            out=bank[:, h, u, :],
                            in_=k_words[:, b * HALVES + h, u * P : (u + 1) * P],
                            identity=ident[:],
                        )
                banks.append(bank)
            for b in range(PAIR):
                nc.scalar.copy(out=k_pairs[:, b], in_=banks[b][:].rearrange("p h u r -> p h r u"))
            k_grouped[i] = k_side

        def project(i):
            q_banks[i] = []
            for g in range(ROW_TILES):
                bank = q_psum.tile([P, PACK, P], F32)
                for t in range(PACK):
                    multiply(
                        bank[:, t, :], w_mx, slice(t * P, (t + 1) * P), x_mx[i], slice(g * P, (g + 1) * P)
                    )
                q_banks[i].append(bank)

        def q_out_of_psum(i):
            q_side = handed.tile([P, COLS * PACK], BF16, align_bytes=64)
            by_tile = q_side[:].rearrange("p (g n t) -> p g n t", g=ROW_TILES, t=PACK)
            for g in range(ROW_TILES):
                nc.vector.scalar_tensor_tensor(
                    out=by_tile[:, g],
                    in0=q_banks[i][g][:].rearrange("p t n -> p n t"),
                    scalar=Q_SCALE,
                    in1=bias_scaled[:].unsqueeze(1).to_broadcast([P, P, PACK]),
                    op0=ALU.mult,
                    op1=ALU.add,
                )
            q_grouped[i] = q_side

        def score(i):
            scores[i] = []
            for b in range(PAIR):
                bank = s_psum.tile([P, HALVES, KEYS], F32)
                for h in range(HALVES):
                    first = b * TOKENS + h * P
                    multiply(
                        bank[:, h, :],
                        q_mx[i],
                        slice(first, first + P),
                        k_mx[i],
                        slice(b * KEYS, (b + 1) * KEYS),
                    )
                scores[i].append(bank)

        def row_maxima(i):
            maxima = handed.tile([P, PAIR, HALVES], F32)
            for b in range(PAIR):
                nc.vector.tensor_reduce(
                    out=maxima[:, b, :],
                    in_=scores[i][b][:],
                    axis=mybir.AxisListType.X,
                    op=ALU.max,
                    negate=True,
                )
            neg_max[i] = maxima

        def exponentials(i):
            e = results.tile([P, PAIR, HALVES, KEYS], F32)
            sums = results.tile([P, PAIR, HALVES], F32)
            for b in range(PAIR):
                for h in range(HALVES):
                    nc.scalar.activation(
                        out=e[:, b, h, :],
                        in_=scores[i][b][:, h, :],
                        func=ACT.Exp,
                        bias=neg_max[i][:, b, h : h + 1],
                        scale=1.0,
                        accum_out=sums[:, b, h : h + 1],
                    )
            probs[i], row_sum[i] = e, sums

        def invert_sums(i):
            inverse = results.tile([P, PAIR, HALVES], F32)
            nc.vector.reciprocal(out=inverse[:], in_=row_sum[i][:])
            inv_sum[i] = inverse

        def normalise_and_store(i):
            engine = nc.vector if i == STEPS - 1 else nc.gpsimd
            for b in range(PAIR):
                for h in range(HALVES):
                    engine.tensor_scalar(
                        out=probs[i][:, b, h, :],
                        in0=probs[i][:, b, h, :],
                        scalar1=inv_sum[i][:, b, h : h + 1],
                        scalar2=0.0,
                        op0=ALU.mult,
                        op1=ALU.add,
                    )
                nc.sync.dma_start(
                    out=out[PAIR * i + b].rearrange("(h r) m -> r h m", r=P), in_=probs[i][:, b]
                )


        w_rows = const.tile([P, PACK * CHANNELS], BF16)
        for u in range(2):
            nc.sync.dma_start(
                out=w_rows[:].rearrange("r (u ec) -> r u ec", u=2)[:, u],
                in_=Wq.rearrange("(u r e) c -> u r (e c)", u=2, e=2)[u],
            )
        for i in range(LOOKAHEAD):
            load(i)
        bias_bf = const.tile([P, PACK], BF16)
        nc.scalar.dma_start(
            out=bias_bf[:].rearrange("r (u e) -> r u e", u=2),
            in_=bq.rearrange("(u r e) -> r u e", u=2, e=2),
        )

        warm = const.tile([P, 1], F32)
        nc.vector.memset(warm[:], 0.0)
        nc.scalar.activation(out=warm[:], in_=warm[:], func=ACT.Exp)

        ident = const.tile([P, P], F32)
        make_identity(nc, ident[:])

        bias_scaled = const.tile([P, PACK], F32)
        nc.vector.tensor_scalar(
            out=bias_scaled[:], in0=bias_bf[:], scalar1=Q_SCALE, scalar2=None, op0=ALU.mult
        )

        w_words = w_rows[:].bitcast(F32).rearrange("r (t p v) -> r t v p", t=PACK, v=2)
        w_side = const.tile([P, PACK * P * PACK], BF16, align_bytes=64)
        w_pairs = w_side[:].bitcast(F32).rearrange("p (t r v) -> p t r v", t=PACK, v=2)
        w_banks = []
        for half in range(2):
            bank = t_psum.tile([P, 2, 2, P], F32)
            for t in range(2):
                for v in range(2):
                    nc.tensor.transpose(
                        out=bank[:, t, v, :], in_=w_words[:, 2 * half + t, v, :], identity=ident[:]
                    )
            w_banks.append(bank)
        for half in range(2):
            nc.vector.tensor_copy(
                out=w_pairs[:, 2 * half : 2 * half + 2, :, :],
                in_=w_banks[half][:].rearrange("p t v r -> p t r v"),
            )
        w_words_mx = const.tile([P, CHANNELS], U32, align_bytes=64)
        w_scales = const.tile([P, CHANNELS], U8, align_bytes=64)
        nc.vector.quantize_mx(out=w_words_mx[:].bitcast(FP8X4), scales=w_scales[:], in_=w_side[:])
        w_mx = (w_words_mx, w_scales)


        def due(i):
            return 0 <= i < STEPS

        for turn in range(STEPS + NORM_LAG):
            if due(turn + LOOKAHEAD):
                load(turn + LOOKAHEAD)
            if due(turn - NORM_LAG):
                invert_sums(turn - NORM_LAG)
                normalise_and_store(turn - NORM_LAG)
            if due(turn):
                regroup_x(turn)
            if due(turn - PROJECT_LAG):
                transpose_k(turn - PROJECT_LAG)
            if due(turn - SCORE_LAG):
                q_out_of_psum(turn - SCORE_LAG)
            if due(turn - SOFTMAX_LAG):
                row_maxima(turn - SOFTMAX_LAG)
                exponentials(turn - SOFTMAX_LAG)
            if due(turn - PROJECT_LAG):
                x_mx[turn - PROJECT_LAG] = quantise(x_grouped[turn - PROJECT_LAG], "x")
                project(turn - PROJECT_LAG)
            if due(turn - SCORE_LAG):
                k_mx[turn - SCORE_LAG] = quantise(k_grouped[turn - SCORE_LAG], "k")
                q_mx[turn - SCORE_LAG] = quantise(q_grouped[turn - SCORE_LAG], "q")
                score(turn - SCORE_LAG)
